import numpy as np
import ml_dtypes


def mxq(x, axis, fmt="e4m3"):
    dtype, down = {"e4m3": (ml_dtypes.float8_e4m3fn, 7), "e5m2": (ml_dtypes.float8_e5m2, 14)}[fmt]
    v = np.moveaxis(np.asarray(x, np.float32).astype(ml_dtypes.bfloat16).astype(np.float64), axis, -1)
    blocks = v.reshape(v.shape[:-1] + (-1, 32))
    amax = np.abs(blocks).max(-1, keepdims=True)
    byte = np.maximum(np.where(amax > 0, np.frexp(amax)[1] - 1 + 127, 0) - down, 1)
    scale = np.exp2(byte - 127.0)
    codes = (blocks / scale).astype(np.float32).astype(dtype).astype(np.float64)
    return np.moveaxis((codes * scale).reshape(v.shape), -1, axis)


WIDE = False


def mx_kscale(k):
    if not WIDE:
        return np.ones(k)
    levels = np.array([10, -10, 5, -5, 0])
    if k % 512:
        return np.exp2(np.random.permutation(np.resize(levels, k // 32))).repeat(32)
    a = np.empty((k // 512, 16))
    for p in range(k // 512):
        a[p, :8] = np.random.permutation(np.resize(levels, 8))
        for g in range(8):
            far = levels[np.abs(levels - a[p, g]) >= 10]
            a[p, g + 8] = far[np.random.randint(len(far))]
    return np.exp2(a.ravel()).repeat(32)


BF16 = ml_dtypes.bfloat16


def bf(x):
    return np.asarray(x, np.float32).astype(BF16)


def f64(x):
    return np.asarray(x).astype(np.float64)


B, IN_DIM, LAT, OUT_DIM = 384, 512, 1024, 512
G = IN_DIM + LAT


def sigmoid(v):
    return 1.0 / (1.0 + np.exp(-v))


def setup_inputs():
    s = mx_kscale(G)
    return {
        "x_t": bf(np.random.standard_normal((B, IN_DIM)) * s[:IN_DIM]),
        "h_t": bf(np.random.standard_normal((B, LAT)) * 0.85 * s[IN_DIM:]),
        "Wy": bf(np.random.standard_normal((G, OUT_DIM)) * 0.8 / np.sqrt(G) / s[:, None]),
        "by": bf(np.random.standard_normal(OUT_DIM) * 0.2),
        "Wo": bf(np.random.standard_normal((G, OUT_DIM)) * 0.8 / np.sqrt(G) / s[:, None]),
        "bo": bf(np.random.standard_normal(OUT_DIM) * 0.2),
    }


def reference(x_t, h_t, Wy, by, Wo, bo):
    xq = mxq(np.concatenate([f64(x_t), f64(h_t)], axis=1), 1, "e4m3")
    y_hat = np.tanh((xq @ mxq(f64(Wy), 0, "e4m3")) + f64(by))
    o_t = sigmoid((xq @ mxq(f64(Wo), 0, "e4m3")) + f64(bo))
    return y_hat * o_t

@@ -1,0 +1,257 @@
+from contextlib import ExitStack
+
+import concourse.mybir as mybir
+from concourse.masks import make_identity
+
+FLOPS = 2 * 384 * 1536 * 1024
+
+F32 = mybir.dt.float32
+BF16 = mybir.dt.bfloat16
+U32 = mybir.dt.uint32
+U8 = mybir.dt.uint8
+I32 = mybir.dt.int32
+FP8X4 = mybir.dt.float8_e4m3fn_x4
+ACT = mybir.ActivationFunctionType
+ALU = mybir.AluOpType
+
+P = 128
+PACK = 4
+K_PASS = P * PACK
+PASSES = 3
+ROWS = 3
+BATCH = ROWS * P
+TILES = 4
+N_OUT = TILES * P
+N_MOVING = 512
+WORDS = K_PASS // 2
+RUN = 4
+TANH = 0
+SIGMOID = 1
+
+X_COLUMNS = {"A": (0, 2 * P), "B": (2 * P, BATCH)}
+X_BANK = {(0, "A"): 4, (0, "B"): 5, (1, "A"): 6, (1, "B"): 7, (2, "A"): 4, (2, "B"): 5}
+BIAS_BANK = 7
+
+
+def tile_gatel0rdcell_pb_kernel(tc, x_t, h_t, Wy, by, Wo, bo, out):
+    nc = tc.nc
+    on_vector = nc.vector.tensor_copy
+    on_scalar = nc.scalar.copy
+    with ExitStack() as ctx:
+        keep = ctx.enter_context(tc.tile_pool(name="keep", bufs=1))
+        psum = ctx.enter_context(tc.psum_pool(name="psum", bufs=1))
+        ctx.enter_context(tc.manual_schedule())
+
+        xt_sb = keep.tile([P, ROWS * K_PASS], BF16, name="xt_sb")
+        ht_sb = keep.tile([P, ROWS * 2 * K_PASS], BF16, name="ht_sb")
+        w_rows = {}
+        w_grouped = {}
+        w_codes = {}
+        w_scales = {}
+        for g in (TANH, SIGMOID):
+            for c in range(PASSES):
+                w_rows[(g, c)] = keep.tile([P, PACK, N_OUT], BF16, name="w_rows%d%d" % (g, c))
+                w_grouped[(g, c)] = keep.tile([P, N_OUT * PACK], BF16, name="w_grouped%d%d" % (g, c), align_bytes=64)
+                w_codes[(g, c)] = keep.tile([P, N_OUT], U32, name="w_codes%d%d" % (g, c), align_bytes=64)
+                w_scales[(g, c)] = keep.tile([P, N_OUT], U8, name="w_scales%d%d" % (g, c), align_bytes=64)
+
+        def load_weights(g, c):
+            rows = (Wy, Wo)[g][c * K_PASS:(c + 1) * K_PASS, :]
+            nc.sync.dma_start(
+                out=w_rows[(g, c)][:],
+                in_=rows.rearrange("(p j) n -> p j n", j=PACK),
+            )
+
+        load_weights(TANH, 0)
+        nc.sync.dma_start(out=xt_sb[:], in_=x_t.rearrange("(p t) k -> p (t k)", t=ROWS))
+        nc.sync.dma_start(out=ht_sb[:], in_=h_t.rearrange("(p t) k -> p (t k)", t=ROWS))
+        load_weights(TANH, 1)
+        load_weights(TANH, 2)
+        load_weights(SIGMOID, 0)
+        load_weights(SIGMOID, 1)
+        load_weights(SIGMOID, 2)
+
+        bias_rows = keep.tile([P, P], BF16, name="bias_rows")
+        nc.vector.memset(bias_rows[:], 0.0)
+        nc.scalar.dma_start(out=bias_rows[0:TILES, :], in_=by.rearrange("(r c) -> r c", c=P))
+        nc.scalar.dma_start(out=bias_rows[TILES:2 * TILES, :], in_=bo.rearrange("(r c) -> r c", c=P))
+        warm = keep.tile([P, 1], F32, name="warm")
+        nc.vector.memset(warm[:], 0.0)
+        nc.scalar.activation(out=warm[:], in_=warm[:], func=ACT.Sigmoid)
+        identity = keep.tile([P, P], F32, name="identity")
+        make_identity(nc, identity[:])
+        x_codes = keep.tile([P, PASSES * N_MOVING], U32, name="x_codes", align_bytes=64)
+        x_scales = keep.tile([P, PASSES * N_MOVING], U8, name="x_scales", align_bytes=64)
+        nc.vector.memset(x_codes[:].bitcast(I32), 0)
+        nc.vector.memset(x_scales[:].bitcast(I32), 0)
+
+        xt_words = xt_sb[:].bitcast(F32)
+        ht_words = ht_sb[:].bitcast(F32)
+        x_grouped = {}
+        for c in range(PASSES):
+            x_grouped[c] = keep.tile([P, BATCH * PACK], BF16, name="x_grouped%d" % c, align_bytes=64)
+        x_psum = {}
+
+        def transpose_x(c, part):
+            lo, hi = X_COLUMNS[part]
+            x_psum[(c, part)] = psum.tile([P, 2, hi - lo], F32, tag="bank%d" % X_BANK[(c, part)], name="x_psum%d%s" % (c, part))
+            for t in range(lo // P, hi // P):
+                for u in range(2):
+                    if c == 0:
+                        first = t * WORDS
+                        words = xt_words[:, first + u:first + WORDS:2]
+                    else:
+                        first = t * 2 * WORDS + (c - 1) * WORDS
+                        words = ht_words[:, first + u:first + WORDS:2]
+                    nc.tensor.transpose(out=x_psum[(c, part)][:, u, t * P - lo:(t + 1) * P - lo], in_=words, identity=identity[:])
+
+        def copy_x(copy, c, part):
+            lo, hi = X_COLUMNS[part]
+            grouped_words = x_grouped[c][:].bitcast(F32).rearrange("p (r u) -> p r u", u=2)
+            copy(out=grouped_words[:, lo:hi, :], in_=x_psum[(c, part)][:].rearrange("p u r -> p r u"))
+
+        def quantise_x(c, part):
+            lo, hi = X_COLUMNS[part]
+            nc.vector.quantize_mx(
+                out=x_codes[:, c * N_MOVING + lo:c * N_MOVING + hi].bitcast(FP8X4),
+                scales=x_scales[:, c * N_MOVING + lo:c * N_MOVING + hi],
+                in_=x_grouped[c][:, lo * PACK:hi * PACK],
+            )
+
+        def regroup(copy, g, c, first_tile, end_tile):
+            lo, hi = first_tile * P, end_tile * P
+            copy(
+                out=w_grouped[(g, c)][:, lo * PACK:hi * PACK].rearrange("p (a i j) -> p a j i", i=RUN, j=PACK),
+                in_=w_rows[(g, c)][:, :, lo:hi].rearrange("p j (a i) -> p a j i", i=RUN),
+            )
+
+        def quantise_weights(g, c, h):
+            lo, hi = h * 2 * P, (h + 1) * 2 * P
+            nc.vector.quantize_mx(
+                out=w_codes[(g, c)][:, lo:hi].bitcast(FP8X4),
+                scales=w_scales[(g, c)][:, lo:hi],
+                in_=w_grouped[(g, c)][:, lo * PACK:hi * PACK],
+            )
+
+        sums = {}
+
+        def multiply(g, c, first_tile, end_tile):
+            for n in range(first_tile, end_tile):
+                if c == 0:
+                    sums[(g, n)] = psum.tile([P, N_MOVING], F32, tag="bank%d" % (g * TILES + n), name="sums%d%d" % (g, n))
+                nc.tensor.matmul_mx(
+                    out=sums[(g, n)][:],
+                    lhsT=w_codes[(g, c)][:, n * P:(n + 1) * P].bitcast(FP8X4),
+                    lhsT_scale=w_scales[(g, c)][:, n * P:(n + 1) * P],
+                    rhs=x_codes[:, c * N_MOVING:(c + 1) * N_MOVING].bitcast(FP8X4),
+                    rhs_scale=x_scales[:, c * N_MOVING:(c + 1) * N_MOVING],
+                    start=(c == 0),
+                    stop=(c == PASSES - 1),
+                )
+
+        bias_rows_f32 = keep.tile([P, P], F32, name="bias_rows_f32")
+        bias = keep.tile([P, 2 * TILES], F32, name="bias")
+        gates = {}
+        products = {}
+        products_psum = {}
+        out_view = out.rearrange("(p t) n -> p t n", t=ROWS)
+
+        def gate(g, n):
+            gates[(g, n)] = keep.tile([P, BATCH], F32, name="gates%d%d" % (g, n))
+            nc.scalar.activation(
+                out=gates[(g, n)][:],
+                in_=sums[(g, n)][:, 0:BATCH],
+                func=(ACT.Tanh, ACT.Sigmoid)[g],
+                bias=bias[:, g * TILES + n:g * TILES + n + 1],
+                scale=1.0,
+            )
+
+        def product(n):
+            products[n] = keep.tile([P, BATCH], F32, name="products%d" % n)
+            nc.vector.tensor_tensor(out=products[n][:], in0=gates[(TANH, n)][:], in1=gates[(SIGMOID, n)][:], op=ALU.mult)
+
+        def transpose_product(n):
+            products_psum[n] = psum.tile([P, ROWS, P], F32, tag="bank%d" % n, name="products_psum%d" % n)
+            for t in range(ROWS):
+                nc.tensor.transpose(out=products_psum[n][:, t, :], in_=products[n][:, t * P:(t + 1) * P], identity=identity[:])
+
+        def store(copy, n):
+            result = keep.tile([P, ROWS, P], F32, name="result%d" % n)
+            copy(out=result[:], in_=products_psum[n][:])
+            nc.sync.dma_start(out=out_view[:, :, n * P:(n + 1) * P], in_=result[:])
+
+
+        regroup(on_scalar, TANH, 0, 0, 1)
+        regroup(on_vector, TANH, 0, 1, 3)
+        regroup(on_scalar, TANH, 0, 3, 4)
+        transpose_x(0, "A")
+        transpose_x(0, "B")
+        quantise_weights(TANH, 0, 0)
+        copy_x(on_vector, 0, "A")
+        copy_x(on_scalar, 0, "B")
+        quantise_weights(TANH, 0, 1)
+        quantise_x(0, "A")
+        quantise_x(0, "B")
+
+        transpose_x(1, "B")
+        transpose_x(2, "B")
+        transpose_x(1, "A")
+        transpose_x(2, "A")
+        copy_x(on_scalar, 1, "B")
+        copy_x(on_scalar, 2, "B")
+        quantise_x(1, "B")
+        regroup(on_vector, TANH, 1, 1, 4)
+        regroup(on_scalar, TANH, 1, 0, 1)
+        copy_x(on_scalar, 1, "A")
+        quantise_x(2, "B")
+        quantise_weights(TANH, 1, 1)
+        regroup(on_scalar, TANH, 2, 1, 2)
+        regroup(on_vector, TANH, 2, 0, 1)
+        quantise_weights(TANH, 1, 0)
+        copy_x(on_scalar, 2, "A")
+        nc.scalar.copy(out=bias_rows_f32[:], in_=bias_rows[:])
+        quantise_x(1, "A")
+        quantise_weights(TANH, 2, 0)
+        regroup(on_scalar, TANH, 2, 2, 3)
+        quantise_x(2, "A")
+        multiply(TANH, 0, 0, TILES)
+        multiply(TANH, 1, 0, TILES)
+        regroup(on_vector, TANH, 2, 3, 4)
+
+        regroup(on_scalar, SIGMOID, 0, 0, 1)
+        regroup(on_vector, SIGMOID, 0, 3, 4)
+        regroup(on_scalar, SIGMOID, 1, 2, 4)
+        quantise_weights(TANH, 2, 1)
+        multiply(TANH, 2, 0, TILES)
+        bias_psum = psum.tile([P, P], F32, tag="bank%d" % BIAS_BANK, name="bias_psum")
+        nc.tensor.transpose(out=bias_psum[:], in_=bias_rows_f32[:], identity=identity[:])
+        regroup(on_vector, SIGMOID, 0, 1, 2)
+        regroup(on_vector, SIGMOID, 1, 0, 2)
+        regroup(on_scalar, SIGMOID, 0, 2, 3)
+        quantise_weights(SIGMOID, 0, 0)
+        quantise_weights(SIGMOID, 1, 0)
+        regroup(on_scalar, SIGMOID, 2, 1, 2)
+        nc.scalar.copy(out=bias[:], in_=bias_psum[:, 0:2 * TILES])
+        quantise_weights(SIGMOID, 0, 1)
+        multiply(SIGMOID, 0, 0, 2)
+        multiply(SIGMOID, 1, 0, 2)
+        multiply(SIGMOID, 0, 2, TILES)
+        regroup(on_vector, SIGMOID, 2, 0, 1)
+        quantise_weights(SIGMOID, 1, 1)
+        quantise_weights(SIGMOID, 2, 0)
+        regroup(on_vector, SIGMOID, 2, 2, 4)
+        for n in range(TILES):
+            gate(TANH, n)
+        multiply(SIGMOID, 2, 0, 2)
+        multiply(SIGMOID, 1, 2, TILES)
+        quantise_weights(SIGMOID, 2, 1)
+        multiply(SIGMOID, 2, 2, TILES)
+
+        for n in range(TILES):
+            gate(SIGMOID, n)
+            product(n)
+            transpose_product(n)
+        store(on_scalar, 0)
+        store(on_scalar, 1)
+        store(on_vector, 2)
+        store(on_vector, 3)

@@ -22,15 +22,15 @@ ROWS = 3
 BATCH = ROWS * P
 TILES = 4
 N_OUT = TILES * P
-N_MOVING = 512
 WORDS = K_PASS // 2
 RUN = 4
 TANH = 0
 SIGMOID = 1
 
-X_COLUMNS = {"A": (0, 2 * P), "B": (2 * P, BATCH)}
-X_BANK = {(0, "A"): 4, (0, "B"): 5, (1, "A"): 6, (1, "B"): 7, (2, "A"): 4, (2, "B"): 5}
-BIAS_BANK = 7
+PARTS = {"A": (0, 2), "B": (2, 3)}
+WIDTH = {"A": 2 * P, "B": P}
+X_START = {(c, part): {"A": 0, "B": PASSES * WIDTH["A"]}[part] + c * WIDTH[part] for c in range(PASSES) for part in "AB"}
+X_WIDTH = PASSES * BATCH
 
 
 def tile_gatel0rdcell_pb_kernel(tc, x_t, h_t, Wy, by, Wo, bo, out):
@@ -42,8 +42,11 @@ def tile_gatel0rdcell_pb_kernel(tc, x_t, h_t, Wy, by, Wo, bo, out):
         psum = ctx.enter_context(tc.psum_pool(name="psum", bufs=1))
         ctx.enter_context(tc.manual_schedule())
 
-        xt_sb = keep.tile([P, ROWS * K_PASS], BF16, name="xt_sb")
-        ht_sb = keep.tile([P, ROWS * 2 * K_PASS], BF16, name="ht_sb")
+        def bank(index, shape, dtype, name):
+            return psum.tile(shape, dtype, tag="bank%d" % index, name=name)
+
+        xt_sb = keep.tile([P, ROWS, K_PASS], BF16, name="xt_sb")
+        ht_sb = keep.tile([P, ROWS, 2 * K_PASS], BF16, name="ht_sb")
         w_rows = {}
         w_grouped = {}
         w_codes = {}
@@ -54,68 +57,82 @@ def tile_gatel0rdcell_pb_kernel(tc, x_t, h_t, Wy, by, Wo, bo, out):
                 w_grouped[(g, c)] = keep.tile([P, N_OUT * PACK], BF16, name="w_grouped%d%d" % (g, c), align_bytes=64)
                 w_codes[(g, c)] = keep.tile([P, N_OUT], U32, name="w_codes%d%d" % (g, c), align_bytes=64)
                 w_scales[(g, c)] = keep.tile([P, N_OUT], U8, name="w_scales%d%d" % (g, c), align_bytes=64)
-
-        def load_weights(g, c):
-            rows = (Wy, Wo)[g][c * K_PASS:(c + 1) * K_PASS, :]
-            nc.sync.dma_start(
-                out=w_rows[(g, c)][:],
-                in_=rows.rearrange("(p j) n -> p j n", j=PACK),
-            )
-
-        load_weights(TANH, 0)
-        nc.sync.dma_start(out=xt_sb[:], in_=x_t.rearrange("(p t) k -> p (t k)", t=ROWS))
-        nc.sync.dma_start(out=ht_sb[:], in_=h_t.rearrange("(p t) k -> p (t k)", t=ROWS))
-        load_weights(TANH, 1)
-        load_weights(TANH, 2)
-        load_weights(SIGMOID, 0)
-        load_weights(SIGMOID, 1)
-        load_weights(SIGMOID, 2)
+        x_grouped = keep.tile([P, X_WIDTH * PACK], BF16, name="x_grouped", align_bytes=64)
+        x_codes = keep.tile([P, X_WIDTH], U32, name="x_codes", align_bytes=64)
+        x_scales = keep.tile([P, X_WIDTH], U8, name="x_scales", align_bytes=64)
 
         bias_rows = keep.tile([P, P], BF16, name="bias_rows")
         nc.vector.memset(bias_rows[:], 0.0)
         nc.scalar.dma_start(out=bias_rows[0:TILES, :], in_=by.rearrange("(r c) -> r c", c=P))
         nc.scalar.dma_start(out=bias_rows[TILES:2 * TILES, :], in_=bo.rearrange("(r c) -> r c", c=P))
+
+        def load_weights(g, c, first_tile=0, end_tile=TILES):
+            rows = (Wy, Wo)[g][c * K_PASS:(c + 1) * K_PASS, :]
+            lo, hi = first_tile * P, end_tile * P
+            nc.sync.dma_start(out=w_rows[(g, c)][:, :, lo:hi], in_=rows.rearrange("(p j) n -> p j n", j=PACK)[:, :, lo:hi])
+
+        def load_h(t):
+            nc.sync.dma_start(out=ht_sb[:, t, :], in_=h_t.rearrange("(p t) k -> p t k", t=ROWS)[:, t, :])
+
+        def load_x():
+            nc.sync.dma_start(out=xt_sb[:], in_=x_t.rearrange("(p t) k -> p t k", t=ROWS))
+
+        load_weights(TANH, 0, 0, 2)
+        load_weights(TANH, 0, 2, 4)
+        load_x()
+        load_weights(TANH, 1)
+        for t in range(ROWS):
+            load_h(t)
+        load_weights(TANH, 2)
+        load_weights(SIGMOID, 0)
+        load_weights(SIGMOID, 1)
+        load_weights(SIGMOID, 2, 0, 2)
+        load_weights(SIGMOID, 2, 2, 4)
+
         warm = keep.tile([P, 1], F32, name="warm")
         nc.vector.memset(warm[:], 0.0)
         nc.scalar.activation(out=warm[:], in_=warm[:], func=ACT.Sigmoid)
         identity = keep.tile([P, P], F32, name="identity")
         make_identity(nc, identity[:])
-        x_codes = keep.tile([P, PASSES * N_MOVING], U32, name="x_codes", align_bytes=64)
-        x_scales = keep.tile([P, PASSES * N_MOVING], U8, name="x_scales", align_bytes=64)
-        nc.vector.memset(x_codes[:].bitcast(I32), 0)
-        nc.vector.memset(x_scales[:].bitcast(I32), 0)
-
-        xt_words = xt_sb[:].bitcast(F32)
-        ht_words = ht_sb[:].bitcast(F32)
-        x_grouped = {}
-        for c in range(PASSES):
-            x_grouped[c] = keep.tile([P, BATCH * PACK], BF16, name="x_grouped%d" % c, align_bytes=64)
+        identity_bf16 = keep.tile([P, P], BF16, name="identity_bf16")
+        make_identity(nc, identity_bf16[:])
+        x_words_out = x_grouped[:].bitcast(F32).rearrange("p (r u) -> p r u", u=2)
         x_psum = {}
 
-        def transpose_x(c, part):
-            lo, hi = X_COLUMNS[part]
-            x_psum[(c, part)] = psum.tile([P, 2, hi - lo], F32, tag="bank%d" % X_BANK[(c, part)], name="x_psum%d%s" % (c, part))
-            for t in range(lo // P, hi // P):
-                for u in range(2):
-                    if c == 0:
-                        first = t * WORDS
-                        words = xt_words[:, first + u:first + WORDS:2]
-                    else:
-                        first = t * 2 * WORDS + (c - 1) * WORDS
-                        words = ht_words[:, first + u:first + WORDS:2]
-                    nc.tensor.transpose(out=x_psum[(c, part)][:, u, t * P - lo:(t + 1) * P - lo], in_=words, identity=identity[:])
+        def transpose_words(out_tile, words):
+            for u in range(2):
+                nc.tensor.transpose(out=out_tile[:, u, :], in_=words[:, u::2], identity=identity[:])
 
-        def copy_x(copy, c, part):
-            lo, hi = X_COLUMNS[part]
-            grouped_words = x_grouped[c][:].bitcast(F32).rearrange("p (r u) -> p r u", u=2)
-            copy(out=grouped_words[:, lo:hi, :], in_=x_psum[(c, part)][:].rearrange("p u r -> p r u"))
+        def transpose_x(index, part):
+            first, end = PARTS[part]
+            x_psum[part] = bank(index, [P, 2, WIDTH[part]], F32, "x_psum" + part)
+            for t in range(first, end):
+                at = (t - first) * P
+                transpose_words(x_psum[part][:, :, at:at + P], xt_sb[:, t, :].bitcast(F32))
 
-        def quantise_x(c, part):
-            lo, hi = X_COLUMNS[part]
+        def copy_x(copy, part):
+            lo = X_START[(0, part)]
+            copy(out=x_words_out[:, lo:lo + WIDTH[part], :], in_=x_psum[part][:].rearrange("p u r -> p r u"))
+
+        h_psum = {}
+
+        def transpose_h(index, t):
+            h_psum[t] = bank(index, [P, 2, 2, P], F32, "h_psum%d" % t)
+            for c in (1, 2):
+                transpose_words(h_psum[t][:, c - 1, :, :], ht_sb[:, t, (c - 1) * K_PASS:c * K_PASS].bitcast(F32))
+
+        def copy_h(copy, t):
+            part = "A" if t < PARTS["A"][1] else "B"
+            lo = X_START[(1, part)]
+            at = (t - PARTS[part][0]) * P
+            passes = x_words_out[:, lo:lo + 2 * WIDTH[part], :].rearrange("p (c r) u -> p c r u", c=2)
+            copy(out=passes[:, :, at:at + P, :], in_=h_psum[t][:].rearrange("p c u r -> p c r u"))
+
+        def quantise_x(part, first_pass, end_pass):
+            lo = X_START[(first_pass, part)]
+            hi = lo + (end_pass - first_pass) * WIDTH[part]
             nc.vector.quantize_mx(
-                out=x_codes[:, c * N_MOVING + lo:c * N_MOVING + hi].bitcast(FP8X4),
-                scales=x_scales[:, c * N_MOVING + lo:c * N_MOVING + hi],
-                in_=x_grouped[c][:, lo * PACK:hi * PACK],
+                out=x_codes[:, lo:hi].bitcast(FP8X4), scales=x_scales[:, lo:hi], in_=x_grouped[:, lo * PACK:hi * PACK]
             )
 
         def regroup(copy, g, c, first_tile, end_tile):
@@ -125,8 +142,27 @@ def tile_gatel0rdcell_pb_kernel(tc, x_t, h_t, Wy, by, Wo, bo, out):
                 in_=w_rows[(g, c)][:, :, lo:hi].rearrange("p j (a i) -> p a j i", i=RUN),
             )
 
-        def quantise_weights(g, c, h):
-            lo, hi = h * 2 * P, (h + 1) * 2 * P
+        w_psum = {}
+
+        def regroup_on_tensor(index, g, c, first_tile, end_tile):
+            count = end_tile - first_tile
+            w_psum[(g, c, first_tile)] = bank(index, [P, count * P * PACK], BF16, "w_psum%d%d%d" % (g, c, first_tile))
+            for n in range(first_tile, end_tile):
+                at = (n - first_tile) * P * PACK
+                nc.tensor.matmul(
+                    out=w_psum[(g, c, first_tile)][:, at:at + P * PACK],
+                    lhsT=identity_bf16[:],
+                    rhs=w_rows[(g, c)][:, :, n * P:(n + 1) * P].rearrange("p j n -> p n j"),
+                    start=True,
+                    stop=True,
+                )
+
+        def copy_w(copy, g, c, first_tile, end_tile):
+            lo, hi = first_tile * P * PACK, end_tile * P * PACK
+            copy(out=w_grouped[(g, c)][:, lo:hi].bitcast(F32), in_=w_psum[(g, c, first_tile)][:].bitcast(F32))
+
+        def quantise_weights(g, c, first_tile, end_tile):
+            lo, hi = first_tile * P, end_tile * P
             nc.vector.quantize_mx(
                 out=w_codes[(g, c)][:, lo:hi].bitcast(FP8X4),
                 scales=w_scales[(g, c)][:, lo:hi],
@@ -135,43 +171,66 @@ def tile_gatel0rdcell_pb_kernel(tc, x_t, h_t, Wy, by, Wo, bo, out):
 
         sums = {}
 
+        def multiply_pass(g, c, n, part):
+            first = X_START[(c, part)]
+            lo, hi = PARTS[part][0] * P, PARTS[part][1] * P
+            nc.tensor.matmul_mx(
+                out=sums[(g, n)][:, lo:hi],
+                lhsT=w_codes[(g, c)][:, n * P:(n + 1) * P].bitcast(FP8X4),
+                lhsT_scale=w_scales[(g, c)][:, n * P:(n + 1) * P],
+                rhs=x_codes[:, first:first + WIDTH[part]].bitcast(FP8X4),
+                rhs_scale=x_scales[:, first:first + WIDTH[part]],
+                start=(c == 0),
+                stop=(c == PASSES - 1),
+            )
+
         def multiply(g, c, first_tile, end_tile):
             for n in range(first_tile, end_tile):
                 if c == 0:
-                    sums[(g, n)] = psum.tile([P, N_MOVING], F32, tag="bank%d" % (g * TILES + n), name="sums%d%d" % (g, n))
-                nc.tensor.matmul_mx(
-                    out=sums[(g, n)][:],
-                    lhsT=w_codes[(g, c)][:, n * P:(n + 1) * P].bitcast(FP8X4),
-                    lhsT_scale=w_scales[(g, c)][:, n * P:(n + 1) * P],
-                    rhs=x_codes[:, c * N_MOVING:(c + 1) * N_MOVING].bitcast(FP8X4),
-                    rhs_scale=x_scales[:, c * N_MOVING:(c + 1) * N_MOVING],
-                    start=(c == 0),
-                    stop=(c == PASSES - 1),
-                )
+                    sums[(g, n)] = bank(g * TILES + n, [P, BATCH], F32, "sums%d%d" % (g, n))
+                multiply_pass(g, c, n, "A")
+                if c == PASSES - 1:
+                    for c_rest in range(PASSES):
+                        multiply_pass(g, c_rest, n, "B")
 
-        bias_rows_f32 = keep.tile([P, P], F32, name="bias_rows_f32")
         bias = keep.tile([P, 2 * TILES], F32, name="bias")
+        bias_psum = {}
         gates = {}
-        products = {}
-        products_psum = {}
+        gates_psum = {}
+        tanh_rows = {}
         out_view = out.rearrange("(p t) n -> p t n", t=ROWS)
+
+        def spread_bias(index):
+            bias_psum[0] = bank(index, [P, 2 * TILES], F32, "bias_psum")
+            nc.tensor.matmul(out=bias_psum[0][:], lhsT=bias_rows[:], rhs=identity_bf16[:, 0:2 * TILES], start=True, stop=True)
+
+        def copy_bias(copy):
+            copy(out=bias[:], in_=bias_psum[0][:])
 
         def gate(g, n):
             gates[(g, n)] = keep.tile([P, BATCH], F32, name="gates%d%d" % (g, n))
             nc.scalar.activation(
                 out=gates[(g, n)][:],
-                in_=sums[(g, n)][:, 0:BATCH],
+                in_=sums[(g, n)][:],
                 func=(ACT.Tanh, ACT.Sigmoid)[g],
                 bias=bias[:, g * TILES + n:g * TILES + n + 1],
                 scale=1.0,
             )
+
+        def transpose_gate(g, n):
+            gates_psum[(g, n)] = bank(g * TILES + n, [P, ROWS, P], F32, "gates_psum%d%d" % (g, n))
+            for t in range(ROWS):
+                nc.tensor.transpose(out=gates_psum[(g, n)][:, t, :], in_=gates[(g, n)][:, t * P:(t + 1) * P], identity=identity[:])
+
+        products = {}
+        products_psum = {}
 
         def product(n):
             products[n] = keep.tile([P, BATCH], F32, name="products%d" % n)
             nc.vector.tensor_tensor(out=products[n][:], in0=gates[(TANH, n)][:], in1=gates[(SIGMOID, n)][:], op=ALU.mult)
 
         def transpose_product(n):
-            products_psum[n] = psum.tile([P, ROWS, P], F32, tag="bank%d" % n, name="products_psum%d" % n)
+            products_psum[n] = bank(n, [P, ROWS, P], F32, "products_psum%d" % n)
             for t in range(ROWS):
                 nc.tensor.transpose(out=products_psum[n][:, t, :], in_=products[n][:, t * P:(t + 1) * P], identity=identity[:])
 
@@ -180,77 +239,86 @@ def tile_gatel0rdcell_pb_kernel(tc, x_t, h_t, Wy, by, Wo, bo, out):
             copy(out=result[:], in_=products_psum[n][:])
             nc.sync.dma_start(out=out_view[:, :, n * P:(n + 1) * P], in_=result[:])
 
+        def keep_tanh(copy, n):
+            tanh_rows[n] = keep.tile([P, ROWS, P], F32, name="tanh_rows%d" % n)
+            copy(out=tanh_rows[n][:], in_=gates_psum[(TANH, n)][:])
 
-        regroup(on_scalar, TANH, 0, 0, 1)
-        regroup(on_vector, TANH, 0, 1, 3)
+        def store_product(n):
+            result = keep.tile([P, ROWS, P], F32, name="result%d" % n)
+            nc.vector.tensor_tensor(out=result[:], in0=gates_psum[(SIGMOID, n)][:], in1=tanh_rows[n][:], op=ALU.mult)
+            nc.sync.dma_start(out=out_view[:, :, n * P:(n + 1) * P], in_=result[:])
+
+        regroup(on_vector, TANH, 0, 0, 2)
         regroup(on_scalar, TANH, 0, 3, 4)
-        transpose_x(0, "A")
-        transpose_x(0, "B")
-        quantise_weights(TANH, 0, 0)
-        copy_x(on_vector, 0, "A")
-        copy_x(on_scalar, 0, "B")
-        quantise_weights(TANH, 0, 1)
-        quantise_x(0, "A")
-        quantise_x(0, "B")
-
-        transpose_x(1, "B")
-        transpose_x(2, "B")
-        transpose_x(1, "A")
-        transpose_x(2, "A")
-        copy_x(on_scalar, 1, "B")
-        copy_x(on_scalar, 2, "B")
-        quantise_x(1, "B")
-        regroup(on_vector, TANH, 1, 1, 4)
-        regroup(on_scalar, TANH, 1, 0, 1)
-        copy_x(on_scalar, 1, "A")
-        quantise_x(2, "B")
-        quantise_weights(TANH, 1, 1)
-        regroup(on_scalar, TANH, 2, 1, 2)
-        regroup(on_vector, TANH, 2, 0, 1)
-        quantise_weights(TANH, 1, 0)
-        copy_x(on_scalar, 2, "A")
-        nc.scalar.copy(out=bias_rows_f32[:], in_=bias_rows[:])
-        quantise_x(1, "A")
-        quantise_weights(TANH, 2, 0)
-        regroup(on_scalar, TANH, 2, 2, 3)
-        quantise_x(2, "A")
+        regroup(on_vector, TANH, 0, 2, 3)
+        quantise_weights(TANH, 0, 0, 2)
+        quantise_weights(TANH, 0, 2, 4)
+        transpose_x(4, "A")
+        transpose_x(5, "B")
+        spread_bias(3)
+        copy_x(on_vector, "A")
+        regroup(on_scalar, TANH, 1, 3, 4)
+        copy_x(on_scalar, "B")
+        copy_bias(on_scalar)
+        regroup(on_vector, TANH, 1, 0, 3)
+        transpose_h(6, 0)
+        transpose_h(7, 1)
+        transpose_h(4, 2)
+        quantise_x("A", 0, 1)
+        quantise_x("B", 0, 1)
+        copy_h(on_scalar, 0)
+        quantise_weights(TANH, 1, 0, 4)
+        copy_h(on_scalar, 1)
+        copy_h(on_scalar, 2)
         multiply(TANH, 0, 0, TILES)
+        regroup_on_tensor(5, TANH, 2, 2, 4)
+        regroup(on_vector, TANH, 2, 0, 2)
+        quantise_x("A", 1, 3)
+        copy_w(on_scalar, TANH, 2, 2, 4)
+        regroup_on_tensor(6, SIGMOID, 0, 2, 4)
+        quantise_x("B", 1, 3)
         multiply(TANH, 1, 0, TILES)
-        regroup(on_vector, TANH, 2, 3, 4)
-
-        regroup(on_scalar, SIGMOID, 0, 0, 1)
-        regroup(on_vector, SIGMOID, 0, 3, 4)
-        regroup(on_scalar, SIGMOID, 1, 2, 4)
-        quantise_weights(TANH, 2, 1)
-        multiply(TANH, 2, 0, TILES)
-        bias_psum = psum.tile([P, P], F32, tag="bank%d" % BIAS_BANK, name="bias_psum")
-        nc.tensor.transpose(out=bias_psum[:], in_=bias_rows_f32[:], identity=identity[:])
-        regroup(on_vector, SIGMOID, 0, 1, 2)
+        quantise_weights(TANH, 2, 0, 2)
+        multiply(TANH, 2, 0, 2)
+        regroup(on_vector, SIGMOID, 0, 0, 2)
+        copy_w(on_scalar, SIGMOID, 0, 2, 4)
+        regroup_on_tensor(7, SIGMOID, 1, 2, 4)
+        quantise_weights(TANH, 2, 2, 4)
+        multiply(TANH, 2, 2, 4)
         regroup(on_vector, SIGMOID, 1, 0, 2)
-        regroup(on_scalar, SIGMOID, 0, 2, 3)
-        quantise_weights(SIGMOID, 0, 0)
-        quantise_weights(SIGMOID, 1, 0)
-        regroup(on_scalar, SIGMOID, 2, 1, 2)
-        nc.scalar.copy(out=bias[:], in_=bias_psum[:, 0:2 * TILES])
-        quantise_weights(SIGMOID, 0, 1)
-        multiply(SIGMOID, 0, 0, 2)
-        multiply(SIGMOID, 1, 0, 2)
-        multiply(SIGMOID, 0, 2, TILES)
-        regroup(on_vector, SIGMOID, 2, 0, 1)
-        quantise_weights(SIGMOID, 1, 1)
-        quantise_weights(SIGMOID, 2, 0)
-        regroup(on_vector, SIGMOID, 2, 2, 4)
-        for n in range(TILES):
-            gate(TANH, n)
-        multiply(SIGMOID, 2, 0, 2)
-        multiply(SIGMOID, 1, 2, TILES)
-        quantise_weights(SIGMOID, 2, 1)
-        multiply(SIGMOID, 2, 2, TILES)
+        gate(TANH, 0)
+        gate(TANH, 1)
 
-        for n in range(TILES):
-            gate(SIGMOID, n)
-            product(n)
-            transpose_product(n)
+        quantise_weights(SIGMOID, 0, 0, 2)
+        multiply(SIGMOID, 0, 0, 2)
+        regroup(on_scalar, SIGMOID, 2, 3, 4)
+        copy_w(on_scalar, SIGMOID, 1, 2, 4)
+        regroup(on_vector, SIGMOID, 2, 0, 2)
+        quantise_weights(SIGMOID, 1, 0, 2)
+        quantise_weights(SIGMOID, 2, 0, 2)
+        multiply(SIGMOID, 1, 0, 2)
+        multiply(SIGMOID, 2, 0, 2)
+        gate(TANH, 2)
+        gate(TANH, 3)
+        quantise_weights(SIGMOID, 0, 2, 4)
+        regroup(on_vector, SIGMOID, 2, 2, 3)
+        quantise_weights(SIGMOID, 1, 2, 4)
+        quantise_weights(SIGMOID, 2, 2, 4)
+        multiply(SIGMOID, 0, 2, 4)
+        multiply(SIGMOID, 1, 2, 4)
+        multiply(SIGMOID, 2, 2, 4)
+        gate(SIGMOID, 0)
+        gate(SIGMOID, 1)
+        product(0)
+        transpose_product(0)
+        product(1)
+        transpose_product(1)
+        gate(SIGMOID, 2)
+        gate(SIGMOID, 3)
+        product(2)
+        transpose_product(2)
+        product(3)
+        transpose_product(3)
         store(on_scalar, 0)
         store(on_scalar, 1)
         store(on_vector, 2)

@@ -142,25 +142,6 @@ def tile_gatel0rdcell_pb_kernel(tc, x_t, h_t, Wy, by, Wo, bo, out):
                 in_=w_rows[(g, c)][:, :, lo:hi].rearrange("p j (a i) -> p a j i", i=RUN),
             )
 
-        w_psum = {}
-
-        def regroup_on_tensor(index, g, c, first_tile, end_tile):
-            count = end_tile - first_tile
-            w_psum[(g, c, first_tile)] = bank(index, [P, count * P * PACK], BF16, "w_psum%d%d%d" % (g, c, first_tile))
-            for n in range(first_tile, end_tile):
-                at = (n - first_tile) * P * PACK
-                nc.tensor.matmul(
-                    out=w_psum[(g, c, first_tile)][:, at:at + P * PACK],
-                    lhsT=identity_bf16[:],
-                    rhs=w_rows[(g, c)][:, :, n * P:(n + 1) * P].rearrange("p j n -> p n j"),
-                    start=True,
-                    stop=True,
-                )
-
-        def copy_w(copy, g, c, first_tile, end_tile):
-            lo, hi = first_tile * P * PACK, end_tile * P * PACK
-            copy(out=w_grouped[(g, c)][:, lo:hi].bitcast(F32), in_=w_psum[(g, c, first_tile)][:].bitcast(F32))
-
         def quantise_weights(g, c, first_tile, end_tile):
             lo, hi = first_tile * P, end_tile * P
             nc.vector.quantize_mx(
@@ -196,8 +177,6 @@ def tile_gatel0rdcell_pb_kernel(tc, x_t, h_t, Wy, by, Wo, bo, out):
         bias = keep.tile([P, 2 * TILES], F32, name="bias")
         bias_psum = {}
         gates = {}
-        gates_psum = {}
-        tanh_rows = {}
         out_view = out.rearrange("(p t) n -> p t n", t=ROWS)
 
         def spread_bias(index):
@@ -217,11 +196,6 @@ def tile_gatel0rdcell_pb_kernel(tc, x_t, h_t, Wy, by, Wo, bo, out):
                 scale=1.0,
             )
 
-        def transpose_gate(g, n):
-            gates_psum[(g, n)] = bank(g * TILES + n, [P, ROWS, P], F32, "gates_psum%d%d" % (g, n))
-            for t in range(ROWS):
-                nc.tensor.transpose(out=gates_psum[(g, n)][:, t, :], in_=gates[(g, n)][:, t * P:(t + 1) * P], identity=identity[:])
-
         products = {}
         products_psum = {}
 
@@ -237,15 +211,6 @@ def tile_gatel0rdcell_pb_kernel(tc, x_t, h_t, Wy, by, Wo, bo, out):
         def store(copy, n):
             result = keep.tile([P, ROWS, P], F32, name="result%d" % n)
             copy(out=result[:], in_=products_psum[n][:])
-            nc.sync.dma_start(out=out_view[:, :, n * P:(n + 1) * P], in_=result[:])
-
-        def keep_tanh(copy, n):
-            tanh_rows[n] = keep.tile([P, ROWS, P], F32, name="tanh_rows%d" % n)
-            copy(out=tanh_rows[n][:], in_=gates_psum[(TANH, n)][:])
-
-        def store_product(n):
-            result = keep.tile([P, ROWS, P], F32, name="result%d" % n)
-            nc.vector.tensor_tensor(out=result[:], in0=gates_psum[(SIGMOID, n)][:], in1=tanh_rows[n][:], op=ALU.mult)
             nc.sync.dma_start(out=out_view[:, :, n * P:(n + 1) * P], in_=result[:])
 
         regroup(on_vector, TANH, 0, 0, 2)
@@ -271,28 +236,25 @@ def tile_gatel0rdcell_pb_kernel(tc, x_t, h_t, Wy, by, Wo, bo, out):
         copy_h(on_scalar, 1)
         copy_h(on_scalar, 2)
         multiply(TANH, 0, 0, TILES)
-        regroup_on_tensor(5, TANH, 2, 2, 4)
-        regroup(on_vector, TANH, 2, 0, 2)
+        regroup(on_vector, TANH, 2, 0, 3)
         quantise_x("A", 1, 3)
-        copy_w(on_scalar, TANH, 2, 2, 4)
-        regroup_on_tensor(6, SIGMOID, 0, 2, 4)
+        regroup(on_scalar, TANH, 2, 3, 4)
         quantise_x("B", 1, 3)
         multiply(TANH, 1, 0, TILES)
         quantise_weights(TANH, 2, 0, 2)
         multiply(TANH, 2, 0, 2)
         regroup(on_vector, SIGMOID, 0, 0, 2)
-        copy_w(on_scalar, SIGMOID, 0, 2, 4)
-        regroup_on_tensor(7, SIGMOID, 1, 2, 4)
+        regroup(on_scalar, SIGMOID, 0, 2, 4)
+        regroup(on_scalar, SIGMOID, 1, 3, 4)
         quantise_weights(TANH, 2, 2, 4)
         multiply(TANH, 2, 2, 4)
-        regroup(on_vector, SIGMOID, 1, 0, 2)
+        regroup(on_vector, SIGMOID, 1, 0, 3)
         gate(TANH, 0)
         gate(TANH, 1)
 
         quantise_weights(SIGMOID, 0, 0, 2)
         multiply(SIGMOID, 0, 0, 2)
         regroup(on_scalar, SIGMOID, 2, 3, 4)
-        copy_w(on_scalar, SIGMOID, 1, 2, 4)
         regroup(on_vector, SIGMOID, 2, 0, 2)
         quantise_weights(SIGMOID, 1, 0, 2)
         quantise_weights(SIGMOID, 2, 0, 2)
@@ -322,4 +284,4 @@ def tile_gatel0rdcell_pb_kernel(tc, x_t, h_t, Wy, by, Wo, bo, out):
         store(on_scalar, 0)
         store(on_scalar, 1)
         store(on_vector, 2)
-        store(on_vector, 3)
+        store(on_scalar, 3)

@@ -23,7 +23,7 @@ BATCH = ROWS * P
 TILES = 4
 N_OUT = TILES * P
 WORDS = K_PASS // 2
-RUN = 4
+RUN = 8
 TANH = 0
 SIGMOID = 1
 

@@ -66,28 +66,24 @@ def tile_gatel0rdcell_pb_kernel(tc, x_t, h_t, Wy, by, Wo, bo, out):
         nc.scalar.dma_start(out=bias_rows[0:TILES, :], in_=by.rearrange("(r c) -> r c", c=P))
         nc.scalar.dma_start(out=bias_rows[TILES:2 * TILES, :], in_=bo.rearrange("(r c) -> r c", c=P))
 
-        def load_weights(g, c, first_tile=0, end_tile=TILES):
+        def load_weights(g, c):
             rows = (Wy, Wo)[g][c * K_PASS:(c + 1) * K_PASS, :]
-            lo, hi = first_tile * P, end_tile * P
-            nc.sync.dma_start(out=w_rows[(g, c)][:, :, lo:hi], in_=rows.rearrange("(p j) n -> p j n", j=PACK)[:, :, lo:hi])
+            nc.sync.dma_start(out=w_rows[(g, c)][:], in_=rows.rearrange("(p j) n -> p j n", j=PACK))
 
-        def load_h(t):
-            nc.sync.dma_start(out=ht_sb[:, t, :], in_=h_t.rearrange("(p t) k -> p t k", t=ROWS)[:, t, :])
+        def load_h():
+            nc.sync.dma_start(out=ht_sb[:], in_=h_t.rearrange("(p t) k -> p t k", t=ROWS))
 
         def load_x():
             nc.sync.dma_start(out=xt_sb[:], in_=x_t.rearrange("(p t) k -> p t k", t=ROWS))
 
-        load_weights(TANH, 0, 0, 2)
-        load_weights(TANH, 0, 2, 4)
+        load_weights(TANH, 0)
         load_x()
         load_weights(TANH, 1)
-        for t in range(ROWS):
-            load_h(t)
+        load_h()
         load_weights(TANH, 2)
         load_weights(SIGMOID, 0)
         load_weights(SIGMOID, 1)
-        load_weights(SIGMOID, 2, 0, 2)
-        load_weights(SIGMOID, 2, 2, 4)
+        load_weights(SIGMOID, 2)
 
         warm = keep.tile([P, 1], F32, name="warm")
         nc.vector.memset(warm[:], 0.0)

@@ -216,11 +216,9 @@ def tile_gatel0rdcell_pb_kernel(tc, x_t, h_t, Wy, by, Wo, bo, out):
         quantise_weights(TANH, 0, 2, 4)
         transpose_x(4, "A")
         transpose_x(5, "B")
-        spread_bias(3)
         copy_x(on_vector, "A")
         regroup(on_scalar, TANH, 1, 3, 4)
         copy_x(on_scalar, "B")
-        copy_bias(on_scalar)
         regroup(on_vector, TANH, 1, 0, 3)
         transpose_h(6, 0)
         transpose_h(7, 1)
@@ -237,6 +235,7 @@ def tile_gatel0rdcell_pb_kernel(tc, x_t, h_t, Wy, by, Wo, bo, out):
         regroup(on_scalar, TANH, 2, 3, 4)
         quantise_x("B", 1, 3)
         multiply(TANH, 1, 0, TILES)
+        spread_bias(5)
         quantise_weights(TANH, 2, 0, 2)
         multiply(TANH, 2, 0, 2)
         regroup(on_vector, SIGMOID, 0, 0, 2)
@@ -245,6 +244,7 @@ def tile_gatel0rdcell_pb_kernel(tc, x_t, h_t, Wy, by, Wo, bo, out):
         quantise_weights(TANH, 2, 2, 4)
         multiply(TANH, 2, 2, 4)
         regroup(on_vector, SIGMOID, 1, 0, 3)
+        copy_bias(on_scalar)
         gate(TANH, 0)
         gate(TANH, 1)
 

from contextlib import ExitStack

import concourse.mybir as mybir
from concourse.masks import make_identity

FLOPS = 2 * 384 * 1536 * 1024

F32 = mybir.dt.float32
BF16 = mybir.dt.bfloat16
U32 = mybir.dt.uint32
U8 = mybir.dt.uint8
I32 = mybir.dt.int32
FP8X4 = mybir.dt.float8_e4m3fn_x4
ACT = mybir.ActivationFunctionType
ALU = mybir.AluOpType

P = 128
PACK = 4
K_PASS = P * PACK
PASSES = 3
ROWS = 3
BATCH = ROWS * P
TILES = 4
N_OUT = TILES * P
WORDS = K_PASS // 2
RUN = 8
TANH = 0
SIGMOID = 1

PARTS = {"A": (0, 2), "B": (2, 3)}
WIDTH = {"A": 2 * P, "B": P}
X_START = {(c, part): {"A": 0, "B": PASSES * WIDTH["A"]}[part] + c * WIDTH[part] for c in range(PASSES) for part in "AB"}
X_WIDTH = PASSES * BATCH


def tile_gatel0rdcell_pb_kernel(tc, x_t, h_t, Wy, by, Wo, bo, out):
    nc = tc.nc
    on_vector = nc.vector.tensor_copy
    on_scalar = nc.scalar.copy
    with ExitStack() as ctx:
        keep = ctx.enter_context(tc.tile_pool(name="keep", bufs=1))
        psum = ctx.enter_context(tc.psum_pool(name="psum", bufs=1))
        ctx.enter_context(tc.manual_schedule())

        def bank(index, shape, dtype, name):
            return psum.tile(shape, dtype, tag="bank%d" % index, name=name)

        xt_sb = keep.tile([P, ROWS, K_PASS], BF16, name="xt_sb")
        ht_sb = keep.tile([P, ROWS, 2 * K_PASS], BF16, name="ht_sb")
        w_rows = {}
        w_grouped = {}
        w_codes = {}
        w_scales = {}
        for g in (TANH, SIGMOID):
            for c in range(PASSES):
                w_rows[(g, c)] = keep.tile([P, PACK, N_OUT], BF16, name="w_rows%d%d" % (g, c))
                w_grouped[(g, c)] = keep.tile([P, N_OUT * PACK], BF16, name="w_grouped%d%d" % (g, c), align_bytes=64)
                w_codes[(g, c)] = keep.tile([P, N_OUT], U32, name="w_codes%d%d" % (g, c), align_bytes=64)
                w_scales[(g, c)] = keep.tile([P, N_OUT], U8, name="w_scales%d%d" % (g, c), align_bytes=64)
        x_grouped = keep.tile([P, X_WIDTH * PACK], BF16, name="x_grouped", align_bytes=64)
        x_codes = keep.tile([P, X_WIDTH], U32, name="x_codes", align_bytes=64)
        x_scales = keep.tile([P, X_WIDTH], U8, name="x_scales", align_bytes=64)

        bias_rows = keep.tile([P, P], BF16, name="bias_rows")
        nc.vector.memset(bias_rows[:], 0.0)
        nc.scalar.dma_start(out=bias_rows[0:TILES, :], in_=by.rearrange("(r c) -> r c", c=P))
        nc.scalar.dma_start(out=bias_rows[TILES:2 * TILES, :], in_=bo.rearrange("(r c) -> r c", c=P))

        def load_weights(g, c):
            rows = (Wy, Wo)[g][c * K_PASS:(c + 1) * K_PASS, :]
            nc.sync.dma_start(out=w_rows[(g, c)][:], in_=rows.rearrange("(p j) n -> p j n", j=PACK))

        def load_h():
            nc.sync.dma_start(out=ht_sb[:], in_=h_t.rearrange("(p t) k -> p t k", t=ROWS))

        def load_x():
            nc.sync.dma_start(out=xt_sb[:], in_=x_t.rearrange("(p t) k -> p t k", t=ROWS))

        load_weights(TANH, 0)
        load_x()
        load_weights(TANH, 1)
        load_h()
        load_weights(TANH, 2)
        load_weights(SIGMOID, 0)
        load_weights(SIGMOID, 1)
        load_weights(SIGMOID, 2)

        warm = keep.tile([P, 1], F32, name="warm")
        nc.vector.memset(warm[:], 0.0)
        nc.scalar.activation(out=warm[:], in_=warm[:], func=ACT.Sigmoid)
        identity = keep.tile([P, P], F32, name="identity")
        make_identity(nc, identity[:])
        identity_bf16 = keep.tile([P, P], BF16, name="identity_bf16")
        make_identity(nc, identity_bf16[:])
        x_words_out = x_grouped[:].bitcast(F32).rearrange("p (r u) -> p r u", u=2)
        x_psum = {}

        def transpose_words(out_tile, words):
            for u in range(2):
                nc.tensor.transpose(out=out_tile[:, u, :], in_=words[:, u::2], identity=identity[:])

        def transpose_x(index, part):
            first, end = PARTS[part]
            x_psum[part] = bank(index, [P, 2, WIDTH[part]], F32, "x_psum" + part)
            for t in range(first, end):
                at = (t - first) * P
                transpose_words(x_psum[part][:, :, at:at + P], xt_sb[:, t, :].bitcast(F32))

        def copy_x(copy, part):
            lo = X_START[(0, part)]
            copy(out=x_words_out[:, lo:lo + WIDTH[part], :], in_=x_psum[part][:].rearrange("p u r -> p r u"))

        h_psum = {}

        def transpose_h(index, t):
            h_psum[t] = bank(index, [P, 2, 2, P], F32, "h_psum%d" % t)
            for c in (1, 2):
                transpose_words(h_psum[t][:, c - 1, :, :], ht_sb[:, t, (c - 1) * K_PASS:c * K_PASS].bitcast(F32))

        def copy_h(copy, t):
            part = "A" if t < PARTS["A"][1] else "B"
            lo = X_START[(1, part)]
            at = (t - PARTS[part][0]) * P
            passes = x_words_out[:, lo:lo + 2 * WIDTH[part], :].rearrange("p (c r) u -> p c r u", c=2)
            copy(out=passes[:, :, at:at + P, :], in_=h_psum[t][:].rearrange("p c u r -> p c r u"))

        def quantise_x(part, first_pass, end_pass):
            lo = X_START[(first_pass, part)]
            hi = lo + (end_pass - first_pass) * WIDTH[part]
            nc.vector.quantize_mx(
                out=x_codes[:, lo:hi].bitcast(FP8X4), scales=x_scales[:, lo:hi], in_=x_grouped[:, lo * PACK:hi * PACK]
            )

        def regroup(copy, g, c, first_tile, end_tile):
            lo, hi = first_tile * P, end_tile * P
            copy(
                out=w_grouped[(g, c)][:, lo * PACK:hi * PACK].rearrange("p (a i j) -> p a j i", i=RUN, j=PACK),
                in_=w_rows[(g, c)][:, :, lo:hi].rearrange("p j (a i) -> p a j i", i=RUN),
            )

        def quantise_weights(g, c, first_tile, end_tile):
            lo, hi = first_tile * P, end_tile * P
            nc.vector.quantize_mx(
                out=w_codes[(g, c)][:, lo:hi].bitcast(FP8X4),
                scales=w_scales[(g, c)][:, lo:hi],
                in_=w_grouped[(g, c)][:, lo * PACK:hi * PACK],
            )

        sums = {}

        def multiply_pass(g, c, n, part):
            first = X_START[(c, part)]
            lo, hi = PARTS[part][0] * P, PARTS[part][1] * P
            nc.tensor.matmul_mx(
                out=sums[(g, n)][:, lo:hi],
                lhsT=w_codes[(g, c)][:, n * P:(n + 1) * P].bitcast(FP8X4),
                lhsT_scale=w_scales[(g, c)][:, n * P:(n + 1) * P],
                rhs=x_codes[:, first:first + WIDTH[part]].bitcast(FP8X4),
                rhs_scale=x_scales[:, first:first + WIDTH[part]],
                start=(c == 0),
                stop=(c == PASSES - 1),
            )

        def multiply(g, c, first_tile, end_tile):
            for n in range(first_tile, end_tile):
                if c == 0:
                    sums[(g, n)] = bank(g * TILES + n, [P, BATCH], F32, "sums%d%d" % (g, n))
                multiply_pass(g, c, n, "A")
                if c == PASSES - 1:
                    for c_rest in range(PASSES):
                        multiply_pass(g, c_rest, n, "B")

        bias = keep.tile([P, 2 * TILES], F32, name="bias")
        bias_psum = {}
        gates = {}
        out_view = out.rearrange("(p t) n -> p t n", t=ROWS)

        def spread_bias(index):
            bias_psum[0] = bank(index, [P, 2 * TILES], F32, "bias_psum")
            nc.tensor.matmul(out=bias_psum[0][:], lhsT=bias_rows[:], rhs=identity_bf16[:, 0:2 * TILES], start=True, stop=True)

        def copy_bias(copy):
            copy(out=bias[:], in_=bias_psum[0][:])

        def gate(g, n):
            gates[(g, n)] = keep.tile([P, BATCH], F32, name="gates%d%d" % (g, n))
            nc.scalar.activation(
                out=gates[(g, n)][:],
                in_=sums[(g, n)][:],
                func=(ACT.Tanh, ACT.Sigmoid)[g],
                bias=bias[:, g * TILES + n:g * TILES + n + 1],
                scale=1.0,
            )

        products = {}
        products_psum = {}

        def product(n):
            products[n] = keep.tile([P, BATCH], F32, name="products%d" % n)
            nc.vector.tensor_tensor(out=products[n][:], in0=gates[(TANH, n)][:], in1=gates[(SIGMOID, n)][:], op=ALU.mult)

        def transpose_product(n):
            products_psum[n] = bank(n, [P, ROWS, P], F32, "products_psum%d" % n)
            for t in range(ROWS):
                nc.tensor.transpose(out=products_psum[n][:, t, :], in_=products[n][:, t * P:(t + 1) * P], identity=identity[:])

        def store(copy, n):
            result = keep.tile([P, ROWS, P], F32, name="result%d" % n)
            copy(out=result[:], in_=products_psum[n][:])
            nc.sync.dma_start(out=out_view[:, :, n * P:(n + 1) * P], in_=result[:])

        regroup(on_vector, TANH, 0, 0, 2)
        regroup(on_scalar, TANH, 0, 3, 4)
        regroup(on_vector, TANH, 0, 2, 3)
        quantise_weights(TANH, 0, 0, 2)
        quantise_weights(TANH, 0, 2, 4)
        transpose_x(4, "A")
        transpose_x(5, "B")
        copy_x(on_vector, "A")
        regroup(on_scalar, TANH, 1, 3, 4)
        copy_x(on_scalar, "B")
        regroup(on_vector, TANH, 1, 0, 3)
        transpose_h(6, 0)
        transpose_h(7, 1)
        transpose_h(4, 2)
        quantise_x("A", 0, 1)
        quantise_x("B", 0, 1)
        copy_h(on_scalar, 0)
        quantise_weights(TANH, 1, 0, 4)
        copy_h(on_scalar, 1)
        copy_h(on_scalar, 2)
        multiply(TANH, 0, 0, TILES)
        regroup(on_vector, TANH, 2, 0, 3)
        quantise_x("A", 1, 3)
        regroup(on_scalar, TANH, 2, 3, 4)
        quantise_x("B", 1, 3)
        multiply(TANH, 1, 0, TILES)
        spread_bias(5)
        quantise_weights(TANH, 2, 0, 2)
        multiply(TANH, 2, 0, 2)
        regroup(on_vector, SIGMOID, 0, 0, 2)
        regroup(on_scalar, SIGMOID, 0, 2, 4)
        regroup(on_scalar, SIGMOID, 1, 3, 4)
        quantise_weights(TANH, 2, 2, 4)
        multiply(TANH, 2, 2, 4)
        regroup(on_vector, SIGMOID, 1, 0, 3)
        copy_bias(on_scalar)
        gate(TANH, 0)
        gate(TANH, 1)

        quantise_weights(SIGMOID, 0, 0, 2)
        multiply(SIGMOID, 0, 0, 2)
        regroup(on_scalar, SIGMOID, 2, 3, 4)
        regroup(on_vector, SIGMOID, 2, 0, 2)
        quantise_weights(SIGMOID, 1, 0, 2)
        quantise_weights(SIGMOID, 2, 0, 2)
        multiply(SIGMOID, 1, 0, 2)
        multiply(SIGMOID, 2, 0, 2)
        gate(TANH, 2)
        gate(TANH, 3)
        quantise_weights(SIGMOID, 0, 2, 4)
        regroup(on_vector, SIGMOID, 2, 2, 3)
        quantise_weights(SIGMOID, 1, 2, 4)
        quantise_weights(SIGMOID, 2, 2, 4)
        multiply(SIGMOID, 0, 2, 4)
        multiply(SIGMOID, 1, 2, 4)
        multiply(SIGMOID, 2, 2, 4)
        gate(SIGMOID, 0)
        gate(SIGMOID, 1)
        product(0)
        transpose_product(0)
        product(1)
        transpose_product(1)
        gate(SIGMOID, 2)
        gate(SIGMOID, 3)
        product(2)
        transpose_product(2)
        product(3)
        transpose_product(3)
        store(on_scalar, 0)
        store(on_scalar, 1)
        store(on_vector, 2)
        store(on_scalar, 3)
